import numpy as np
import ml_dtypes

BF16 = ml_dtypes.bfloat16


def bf(x):
    return np.asarray(x, np.float32).astype(BF16)


def f32(x):
    return np.asarray(x, np.float32)


def f64(x):
    return np.asarray(x).astype(np.float64)


def striped(idx):
    return np.tile(idx.reshape(-1, 16).T, (8, 1))


C, S, H, K, N = 256, 256, 128, 4, 512
EPS = 1e-5


def setup_inputs():
    idx = np.concatenate([np.random.permutation(S)[:H] for _ in range(K)])
    return {"table": f32(np.random.standard_normal((C, S))), "pos": f32(np.random.standard_normal((C, N))), "gain": f32(1.0 + 0.1 * np.random.standard_normal((C, 1))), "bias": f32(0.1 * np.random.standard_normal((C, 1))), "offs": striped(idx)}


def reference(table, pos, gain, bias, offs):
    idx = offs[:16].T.reshape(-1)
    x = f64(table)[:, idx] + f64(pos)
    mu = x.mean(axis=0, keepdims=True)
    var = np.square(x - mu).mean(axis=0, keepdims=True)
    return (x - mu) / np.sqrt(var + EPS) * f64(gain) + f64(bias)

@@ -1,0 +1,96 @@
+import concourse.masks as masks
+import concourse.mybir as mybir
+
+F32 = mybir.dt.float32
+U16 = mybir.dt.uint16
+ADD = mybir.AluOpType.add
+MULT = mybir.AluOpType.mult
+IDENTITY = mybir.ActivationFunctionType.Identity
+SQRT = mybir.ActivationFunctionType.Sqrt
+
+P = 128
+C = 256
+S = 256
+N = 512
+EPS = 1e-5
+FEATURE_BLOCKS = C // P
+TOKEN_BLOCKS = N // P
+OFFSET_COLUMNS = P // 16
+
+
+def tile_bitmarmodel_kernel(tc, table, pos, gain, bias, offs, out):
+    nc = tc.nc
+
+    pos_view = pos.rearrange("(b p) n -> p b n", p=P)
+    out_view = out.rearrange("(b p) n -> p b n", p=P)
+    gain_view = gain.rearrange("(b p) o -> p (b o)", p=P)
+    bias_view = bias.rearrange("(b p) o -> p (b o)", p=P)
+
+    with (
+        tc.tile_pool(name="held", bufs=1) as held,
+        tc.tile_pool(name="work", bufs=TOKEN_BLOCKS) as work,
+        tc.psum_pool(name="psum", bufs=TOKEN_BLOCKS) as psum,
+    ):
+        identity = held.tile([P, P], F32, name="identity")
+        masks.make_identity(nc, identity[:])
+        eps = held.tile([P, 1], F32, name="eps")
+        nc.vector.memset(eps[:], EPS)
+
+        offsets = held.tile([P, N // 16], U16, name="offsets")
+        nc.sync.dma_start(offsets[:], offs)
+        windows = []
+        for b, queue in zip(range(FEATURE_BLOCKS), (nc.scalar, nc.sync)):
+            window = held.tile([P, S], F32, name=f"window{b}")
+            queue.dma_start(window[:], table[b * P : (b + 1) * P, :])
+            windows.append(window)
+        pos_blocks = []
+        for t in range(TOKEN_BLOCKS):
+            pos_block = work.tile([P, FEATURE_BLOCKS, P], F32, name="pos_block")
+            queue = nc.scalar if t % 2 == 0 else nc.sync
+            queue.dma_start(pos_block[:], pos_view[:, :, t * P : (t + 1) * P])
+            pos_blocks.append(pos_block)
+        gain_sb = held.tile([P, FEATURE_BLOCKS], F32, name="gain_sb")
+        bias_sb = held.tile([P, FEATURE_BLOCKS], F32, name="bias_sb")
+        with nc.allow_non_contiguous_dma(reason="256 numbers, one to a partition and feature block"):
+            nc.gpsimd.dma_start(gain_sb[:], gain_view)
+            nc.gpsimd.dma_start(bias_sb[:], bias_view)
+
+        for t in range(TOKEN_BLOCKS):
+            x = work.tile([P, FEATURE_BLOCKS, P], F32, name="x")
+            piece = offsets[:, t * OFFSET_COLUMNS : (t + 1) * OFFSET_COLUMNS]
+            for b in range(FEATURE_BLOCKS):
+                nc.vector.tensor_tensor(
+                    x[:, b, :], windows[b][:].indirect(piece), pos_blocks[t][:, b, :], ADD
+                )
+
+            x_turned = psum.tile([P, C], F32, name="x_turned")
+            for b in range(FEATURE_BLOCKS):
+                nc.tensor.transpose(x_turned[:, b * P : (b + 1) * P], x[:, b, :], identity[:])
+
+            stats = work.tile([P, 6], F32, name="stats")
+            nc.vector.bn_stats(stats[:], x_turned[:])
+            mean_var = work.tile([P, 2], F32, name="mean_var")
+            nc.vector.bn_aggr(mean_var[:], stats[:])
+
+            std = work.tile([P, 1], F32, name="std")
+            nc.scalar.activation(std[:], mean_var[:, 1:2], SQRT, bias=eps[:])
+            rstd = work.tile([P, 1], F32, name="rstd")
+            nc.vector.reciprocal(rstd[:], std[:])
+            shift = work.tile([P, 1], F32, name="shift")
+            nc.vector.tensor_scalar(shift[:], mean_var[:, 0:1], rstd[:], -1.0, MULT, MULT)
+
+            y = work.tile([P, C], F32, name="y")
+            nc.scalar.activation(y[:], x_turned[:], IDENTITY, bias=shift[:], scale=rstd[:])
+
+            y_turned = psum.tile([P, FEATURE_BLOCKS, P], F32, name="y_turned")
+            result = work.tile([P, FEATURE_BLOCKS, P], F32, name="result")
+            for b in range(FEATURE_BLOCKS):
+                nc.tensor.transpose(y_turned[:, b, :], y[:, b * P : (b + 1) * P], identity[:])
+                nc.scalar.activation(
+                    result[:, b, :],
+                    y_turned[:, b, :],
+                    IDENTITY,
+                    bias=bias_sb[:, b : b + 1],
+                    scale=gain_sb[:, b : b + 1],
+                )
+            nc.sync.dma_start(out_view[:, :, t * P : (t + 1) * P], result[:])

@@ -23,13 +23,14 @@ def tile_bitmarmodel_kernel(tc, table, pos, gain, bias, offs, out):
 
     pos_view = pos.rearrange("(b p) n -> p b n", p=P)
     out_view = out.rearrange("(b p) n -> p b n", p=P)
-    gain_view = gain.rearrange("(b p) o -> p (b o)", p=P)
-    bias_view = bias.rearrange("(b p) o -> p (b o)", p=P)
+    gain_rows = gain.rearrange("(b p) o -> b (p o)", p=P)
+    bias_rows = bias.rearrange("(b p) o -> b (p o)", p=P)
 
     with (
         tc.tile_pool(name="held", bufs=1) as held,
         tc.tile_pool(name="work", bufs=TOKEN_BLOCKS) as work,
-        tc.psum_pool(name="psum", bufs=TOKEN_BLOCKS) as psum,
+        tc.psum_pool(name="psum_once", bufs=1) as psum_once,
+        tc.psum_pool(name="psum", bufs=3) as psum,
     ):
         identity = held.tile([P, P], F32, name="identity")
         masks.make_identity(nc, identity[:])
@@ -49,11 +50,16 @@ def tile_bitmarmodel_kernel(tc, table, pos, gain, bias, offs, out):
             queue = nc.scalar if t % 2 == 0 else nc.sync
             queue.dma_start(pos_block[:], pos_view[:, :, t * P : (t + 1) * P])
             pos_blocks.append(pos_block)
-        gain_sb = held.tile([P, FEATURE_BLOCKS], F32, name="gain_sb")
-        bias_sb = held.tile([P, FEATURE_BLOCKS], F32, name="bias_sb")
-        with nc.allow_non_contiguous_dma(reason="256 numbers, one to a partition and feature block"):
-            nc.gpsimd.dma_start(gain_sb[:], gain_view)
-            nc.gpsimd.dma_start(bias_sb[:], bias_view)
+        rows = held.tile([2 * FEATURE_BLOCKS, P], F32, name="rows")
+        nc.scalar.dma_start(rows[0:FEATURE_BLOCKS, :], gain_rows)
+        nc.sync.dma_start(rows[FEATURE_BLOCKS : 2 * FEATURE_BLOCKS, :], bias_rows)
+
+        columns_psum = psum_once.tile([P, 2 * FEATURE_BLOCKS], F32, name="columns_psum")
+        nc.tensor.matmul(
+            columns_psum[:], rows[:], identity[0 : 2 * FEATURE_BLOCKS, 0 : 2 * FEATURE_BLOCKS]
+        )
+        columns = held.tile([P, 2 * FEATURE_BLOCKS], F32, name="columns")
+        nc.vector.tensor_copy(columns[:], columns_psum[:])
 
         for t in range(TOKEN_BLOCKS):
             x = work.tile([P, FEATURE_BLOCKS, P], F32, name="x")
@@ -90,7 +96,7 @@ def tile_bitmarmodel_kernel(tc, table, pos, gain, bias, offs, out):
                     result[:, b, :],
                     y_turned[:, b, :],
                     IDENTITY,
-                    bias=bias_sb[:, b : b + 1],
-                    scale=gain_sb[:, b : b + 1],
+                    bias=columns[:, FEATURE_BLOCKS + b : FEATURE_BLOCKS + b + 1],
+                    scale=columns[:, b : b + 1],
                 )
             nc.sync.dma_start(out_view[:, :, t * P : (t + 1) * P], result[:])

@@ -5,8 +5,9 @@ F32 = mybir.dt.float32
 U16 = mybir.dt.uint16
 ADD = mybir.AluOpType.add
 MULT = mybir.AluOpType.mult
+SUBTRACT = mybir.AluOpType.subtract
 IDENTITY = mybir.ActivationFunctionType.Identity
-SQRT = mybir.ActivationFunctionType.Sqrt
+ABS_RECIPROCAL_SQRT = mybir.ActivationFunctionType.Abs_reciprocal_sqrt
 
 P = 128
 C = 256
@@ -23,14 +24,13 @@ def tile_bitmarmodel_kernel(tc, table, pos, gain, bias, offs, out):
 
     pos_view = pos.rearrange("(b p) n -> p b n", p=P)
     out_view = out.rearrange("(b p) n -> p b n", p=P)
-    gain_rows = gain.rearrange("(b p) o -> b (p o)", p=P)
-    bias_rows = bias.rearrange("(b p) o -> b (p o)", p=P)
+    gain_view = gain.rearrange("(b p) o -> p (b o)", p=P)
+    bias_view = bias.rearrange("(b p) o -> p (b o)", p=P)
 
     with (
         tc.tile_pool(name="held", bufs=1) as held,
         tc.tile_pool(name="work", bufs=TOKEN_BLOCKS) as work,
-        tc.psum_pool(name="psum_once", bufs=1) as psum_once,
-        tc.psum_pool(name="psum", bufs=3) as psum,
+        tc.psum_pool(name="psum", bufs=TOKEN_BLOCKS) as psum,
     ):
         identity = held.tile([P, P], F32, name="identity")
         masks.make_identity(nc, identity[:])
@@ -40,26 +40,20 @@ def tile_bitmarmodel_kernel(tc, table, pos, gain, bias, offs, out):
         offsets = held.tile([P, N // 16], U16, name="offsets")
         nc.sync.dma_start(offsets[:], offs)
         windows = []
-        for b, queue in zip(range(FEATURE_BLOCKS), (nc.scalar, nc.sync)):
+        for b in range(FEATURE_BLOCKS):
             window = held.tile([P, S], F32, name=f"window{b}")
-            queue.dma_start(window[:], table[b * P : (b + 1) * P, :])
+            nc.sync.dma_start(window[:], table[b * P : (b + 1) * P, :])
             windows.append(window)
         pos_blocks = []
         for t in range(TOKEN_BLOCKS):
             pos_block = work.tile([P, FEATURE_BLOCKS, P], F32, name="pos_block")
-            queue = nc.scalar if t % 2 == 0 else nc.sync
-            queue.dma_start(pos_block[:], pos_view[:, :, t * P : (t + 1) * P])
+            nc.scalar.dma_start(pos_block[:], pos_view[:, :, t * P : (t + 1) * P])
             pos_blocks.append(pos_block)
-        rows = held.tile([2 * FEATURE_BLOCKS, P], F32, name="rows")
-        nc.scalar.dma_start(rows[0:FEATURE_BLOCKS, :], gain_rows)
-        nc.sync.dma_start(rows[FEATURE_BLOCKS : 2 * FEATURE_BLOCKS, :], bias_rows)
-
-        columns_psum = psum_once.tile([P, 2 * FEATURE_BLOCKS], F32, name="columns_psum")
-        nc.tensor.matmul(
-            columns_psum[:], rows[:], identity[0 : 2 * FEATURE_BLOCKS, 0 : 2 * FEATURE_BLOCKS]
-        )
-        columns = held.tile([P, 2 * FEATURE_BLOCKS], F32, name="columns")
-        nc.vector.tensor_copy(columns[:], columns_psum[:])
+        gain_sb = held.tile([P, FEATURE_BLOCKS], F32, name="gain_sb")
+        bias_sb = held.tile([P, FEATURE_BLOCKS], F32, name="bias_sb")
+        with nc.allow_non_contiguous_dma(reason="256 numbers, one to a partition and feature block"):
+            nc.sync.dma_start(gain_sb[:], gain_view)
+            nc.sync.dma_start(bias_sb[:], bias_view)
 
         for t in range(TOKEN_BLOCKS):
             x = work.tile([P, FEATURE_BLOCKS, P], F32, name="x")
@@ -78,25 +72,22 @@ def tile_bitmarmodel_kernel(tc, table, pos, gain, bias, offs, out):
             mean_var = work.tile([P, 2], F32, name="mean_var")
             nc.vector.bn_aggr(mean_var[:], stats[:])
 
-            std = work.tile([P, 1], F32, name="std")
-            nc.scalar.activation(std[:], mean_var[:, 1:2], SQRT, bias=eps[:])
             rstd = work.tile([P, 1], F32, name="rstd")
-            nc.vector.reciprocal(rstd[:], std[:])
-            shift = work.tile([P, 1], F32, name="shift")
-            nc.vector.tensor_scalar(shift[:], mean_var[:, 0:1], rstd[:], -1.0, MULT, MULT)
+            nc.scalar.activation(rstd[:], mean_var[:, 1:2], ABS_RECIPROCAL_SQRT, bias=eps[:])
 
             y = work.tile([P, C], F32, name="y")
-            nc.scalar.activation(y[:], x_turned[:], IDENTITY, bias=shift[:], scale=rstd[:])
+            nc.vector.tensor_scalar(y[:], x_turned[:], mean_var[:, 0:1], rstd[:], SUBTRACT, MULT)
 
             y_turned = psum.tile([P, FEATURE_BLOCKS, P], F32, name="y_turned")
             result = work.tile([P, FEATURE_BLOCKS, P], F32, name="result")
             for b in range(FEATURE_BLOCKS):
                 nc.tensor.transpose(y_turned[:, b, :], y[:, b * P : (b + 1) * P], identity[:])
+            for b in range(FEATURE_BLOCKS):
                 nc.scalar.activation(
                     result[:, b, :],
                     y_turned[:, b, :],
                     IDENTITY,
-                    bias=columns[:, FEATURE_BLOCKS + b : FEATURE_BLOCKS + b + 1],
-                    scale=columns[:, b : b + 1],
+                    bias=bias_sb[:, b : b + 1],
+                    scale=gain_sb[:, b : b + 1],
                 )
             nc.sync.dma_start(out_view[:, :, t * P : (t + 1) * P], result[:])

@@ -5,9 +5,9 @@ F32 = mybir.dt.float32
 U16 = mybir.dt.uint16
 ADD = mybir.AluOpType.add
 MULT = mybir.AluOpType.mult
-SUBTRACT = mybir.AluOpType.subtract
 IDENTITY = mybir.ActivationFunctionType.Identity
 ABS_RECIPROCAL_SQRT = mybir.ActivationFunctionType.Abs_reciprocal_sqrt
+SQUARE = mybir.ActivationFunctionType.Square
 
 P = 128
 C = 256
@@ -36,6 +36,8 @@ def tile_bitmarmodel_kernel(tc, table, pos, gain, bias, offs, out):
         masks.make_identity(nc, identity[:])
         eps = held.tile([P, 1], F32, name="eps")
         nc.vector.memset(eps[:], EPS)
+        table_warm_up = held.tile([P, 1], F32, name="table_warm_up")
+        nc.scalar.activation(table_warm_up[:], eps[:], ABS_RECIPROCAL_SQRT)
 
         offsets = held.tile([P, N // 16], U16, name="offsets")
         nc.sync.dma_start(offsets[:], offs)
@@ -67,16 +69,17 @@ def tile_bitmarmodel_kernel(tc, table, pos, gain, bias, offs, out):
             for b in range(FEATURE_BLOCKS):
                 nc.tensor.transpose(x_turned[:, b * P : (b + 1) * P], x[:, b, :], identity[:])
 
-            stats = work.tile([P, 6], F32, name="stats")
-            nc.vector.bn_stats(stats[:], x_turned[:])
-            mean_var = work.tile([P, 2], F32, name="mean_var")
-            nc.vector.bn_aggr(mean_var[:], stats[:])
-
+            unused = work.tile([P, C], F32, name="unused")
+            neg_mean = work.tile([P, 1], F32, name="neg_mean")
+            nc.scalar.activation(unused[:], x_turned[:], IDENTITY, scale=-1.0 / C, accum_out=neg_mean[:])
+            squares = work.tile([P, C], F32, name="squares")
+            sum_squares = work.tile([P, 1], F32, name="sum_squares")
+            nc.scalar.activation(squares[:], x_turned[:], SQUARE, bias=neg_mean[:], accum_out=sum_squares[:])
             rstd = work.tile([P, 1], F32, name="rstd")
-            nc.scalar.activation(rstd[:], mean_var[:, 1:2], ABS_RECIPROCAL_SQRT, bias=eps[:])
+            nc.scalar.activation(rstd[:], sum_squares[:], ABS_RECIPROCAL_SQRT, bias=eps[:], scale=1.0 / C)
 
             y = work.tile([P, C], F32, name="y")
-            nc.vector.tensor_scalar(y[:], x_turned[:], mean_var[:, 0:1], rstd[:], SUBTRACT, MULT)
+            nc.vector.tensor_scalar(y[:], x_turned[:], neg_mean[:], rstd[:], ADD, MULT)
 
             y_turned = psum.tile([P, FEATURE_BLOCKS, P], F32, name="y_turned")
             result = work.tile([P, FEATURE_BLOCKS, P], F32, name="result")

@@ -5,6 +5,7 @@ F32 = mybir.dt.float32
 U16 = mybir.dt.uint16
 ADD = mybir.AluOpType.add
 MULT = mybir.AluOpType.mult
+SUBTRACT = mybir.AluOpType.subtract
 IDENTITY = mybir.ActivationFunctionType.Identity
 ABS_RECIPROCAL_SQRT = mybir.ActivationFunctionType.Abs_reciprocal_sqrt
 SQUARE = mybir.ActivationFunctionType.Square
@@ -30,7 +31,7 @@ def tile_bitmarmodel_kernel(tc, table, pos, gain, bias, offs, out):
     with (
         tc.tile_pool(name="held", bufs=1) as held,
         tc.tile_pool(name="work", bufs=TOKEN_BLOCKS) as work,
-        tc.psum_pool(name="psum", bufs=TOKEN_BLOCKS) as psum,
+        tc.psum_pool(name="psum", bufs=2) as psum,
     ):
         identity = held.tile([P, P], F32, name="identity")
         masks.make_identity(nc, identity[:])
@@ -65,32 +66,41 @@ def tile_bitmarmodel_kernel(tc, table, pos, gain, bias, offs, out):
                     x[:, b, :], windows[b][:].indirect(piece), pos_blocks[t][:, b, :], ADD
                 )
 
-            x_turned = psum.tile([P, C], F32, name="x_turned")
+            x_turned = psum.tile([P, C], F32, name="x_turned", bufs=TOKEN_BLOCKS)
             for b in range(FEATURE_BLOCKS):
                 nc.tensor.transpose(x_turned[:, b * P : (b + 1) * P], x[:, b, :], identity[:])
 
-            unused = work.tile([P, C], F32, name="unused")
-            neg_mean = work.tile([P, 1], F32, name="neg_mean")
-            nc.scalar.activation(unused[:], x_turned[:], IDENTITY, scale=-1.0 / C, accum_out=neg_mean[:])
-            squares = work.tile([P, C], F32, name="squares")
-            sum_squares = work.tile([P, 1], F32, name="sum_squares")
-            nc.scalar.activation(squares[:], x_turned[:], SQUARE, bias=neg_mean[:], accum_out=sum_squares[:])
-            rstd = work.tile([P, 1], F32, name="rstd")
-            nc.scalar.activation(rstd[:], sum_squares[:], ABS_RECIPROCAL_SQRT, bias=eps[:], scale=1.0 / C)
-
             y = work.tile([P, C], F32, name="y")
-            nc.vector.tensor_scalar(y[:], x_turned[:], neg_mean[:], rstd[:], ADD, MULT)
+            if t == 0:
+                small = held.tile([P, 2], F32, name="small", tag="rstd")
+                rstd, shift = small[:, 0:1], small[:, 1:2]
+                unused = work.tile([P, C], F32, name="unused")
+                neg_mean = work.tile([P, 1], F32, name="neg_mean")
+                nc.scalar.activation(unused[:], x_turned[:], IDENTITY, scale=-1.0 / C, accum_out=neg_mean[:])
+                squares = work.tile([P, C], F32, name="squares")
+                sum_squares = work.tile([P, 1], F32, name="sum_squares")
+                nc.scalar.activation(squares[:], x_turned[:], SQUARE, bias=neg_mean[:], accum_out=sum_squares[:])
+                nc.scalar.activation(rstd, sum_squares[:], ABS_RECIPROCAL_SQRT, bias=eps[:], scale=1.0 / C)
+                nc.scalar.activation(shift, neg_mean[:], IDENTITY, scale=rstd)
+                nc.scalar.activation(y[:], x_turned[:], IDENTITY, bias=shift, scale=rstd)
+            else:
+                if t == 1:
+                    rstds = held.tile([P, TOKEN_BLOCKS - 1], F32, name="rstds", tag="rstd")
+                rstd = rstds[:, t - 1 : t]
+                stats = work.tile([P, 6], F32, name="stats")
+                nc.vector.bn_stats(stats[:], x_turned[:])
+                mean_var = work.tile([P, 2], F32, name="mean_var")
+                nc.vector.bn_aggr(mean_var[:], stats[:])
+                nc.scalar.activation(rstd, mean_var[:, 1:2], ABS_RECIPROCAL_SQRT, bias=eps[:])
+                nc.vector.tensor_scalar(y[:], x_turned[:], mean_var[:, 0:1], rstd, SUBTRACT, MULT)
 
-            y_turned = psum.tile([P, FEATURE_BLOCKS, P], F32, name="y_turned")
             result = work.tile([P, FEATURE_BLOCKS, P], F32, name="result")
             for b in range(FEATURE_BLOCKS):
-                nc.tensor.transpose(y_turned[:, b, :], y[:, b * P : (b + 1) * P], identity[:])
-            for b in range(FEATURE_BLOCKS):
-                nc.scalar.activation(
-                    result[:, b, :],
-                    y_turned[:, b, :],
-                    IDENTITY,
-                    bias=bias_sb[:, b : b + 1],
-                    scale=gain_sb[:, b : b + 1],
-                )
+                y_turned = psum.tile([P, P], F32, name=f"y_turned{b}", bufs=2)
+                nc.tensor.transpose(y_turned[:], y[:, b * P : (b + 1) * P], identity[:])
+                gain_b, bias_b = gain_sb[:, b : b + 1], bias_sb[:, b : b + 1]
+                if t < TOKEN_BLOCKS // 2 or b == 0:
+                    nc.scalar.activation(result[:, b, :], y_turned[:], IDENTITY, bias=bias_b, scale=gain_b)
+                else:
+                    nc.vector.tensor_scalar(result[:, b, :], y_turned[:], gain_b, bias_b, MULT, ADD)
             nc.sync.dma_start(out_view[:, :, t * P : (t + 1) * P], result[:])

@@ -18,6 +18,7 @@ EPS = 1e-5
 FEATURE_BLOCKS = C // P
 TOKEN_BLOCKS = N // P
 OFFSET_COLUMNS = P // 16
+PIECES = ((0, 1), (1, TOKEN_BLOCKS - 1), (TOKEN_BLOCKS - 1, TOKEN_BLOCKS))
 
 
 def tile_bitmarmodel_kernel(tc, table, pos, gain, bias, offs, out):
@@ -43,29 +44,32 @@ def tile_bitmarmodel_kernel(tc, table, pos, gain, bias, offs, out):
         offsets = held.tile([P, N // 16], U16, name="offsets")
         nc.sync.dma_start(offsets[:], offs)
         windows = []
-        for b in range(FEATURE_BLOCKS):
-            window = held.tile([P, S], F32, name=f"window{b}")
-            nc.sync.dma_start(window[:], table[b * P : (b + 1) * P, :])
-            windows.append(window)
-        pos_blocks = []
-        for t in range(TOKEN_BLOCKS):
-            pos_block = work.tile([P, FEATURE_BLOCKS, P], F32, name="pos_block")
-            nc.scalar.dma_start(pos_block[:], pos_view[:, :, t * P : (t + 1) * P])
-            pos_blocks.append(pos_block)
+        pos_parts = {}
+        for first, end in PIECES:
+            for b in range(FEATURE_BLOCKS):
+                if first == 0:
+                    window = held.tile([P, S], F32, name=f"window{b}")
+                    nc.sync.dma_start(window[:], table[b * P : (b + 1) * P, :])
+                    windows.append(window)
+                pos_part = held.tile([P, (end - first) * P], F32, name=f"pos{first}_{b}")
+                nc.sync.dma_start(pos_part[:], pos_view[:, b, first * P : end * P])
+                pos_parts[first, b] = pos_part
         gain_sb = held.tile([P, FEATURE_BLOCKS], F32, name="gain_sb")
         bias_sb = held.tile([P, FEATURE_BLOCKS], F32, name="bias_sb")
         with nc.allow_non_contiguous_dma(reason="256 numbers, one to a partition and feature block"):
             nc.sync.dma_start(gain_sb[:], gain_view)
             nc.sync.dma_start(bias_sb[:], bias_view)
 
-        for t in range(TOKEN_BLOCKS):
-            x = work.tile([P, FEATURE_BLOCKS, P], F32, name="x")
-            piece = offsets[:, t * OFFSET_COLUMNS : (t + 1) * OFFSET_COLUMNS]
+        x_blocks = []
+        for first, end in PIECES:
+            x = held.tile([P, FEATURE_BLOCKS, (end - first) * P], F32, name=f"x{first}")
+            piece = offsets[:, first * OFFSET_COLUMNS : end * OFFSET_COLUMNS]
             for b in range(FEATURE_BLOCKS):
-                nc.vector.tensor_tensor(
-                    x[:, b, :], windows[b][:].indirect(piece), pos_blocks[t][:, b, :], ADD
-                )
+                nc.vector.tensor_tensor(x[:, b, :], windows[b][:].indirect(piece), pos_parts[first, b][:], ADD)
+            x_blocks += [x[:, :, i * P : (i + 1) * P] for i in range(end - first)]
 
+        for t in range(TOKEN_BLOCKS):
+            x = x_blocks[t]
             x_turned = psum.tile([P, C], F32, name="x_turned", bufs=TOKEN_BLOCKS)
             for b in range(FEATURE_BLOCKS):
                 nc.tensor.transpose(x_turned[:, b * P : (b + 1) * P], x[:, b, :], identity[:])

@@ -32,7 +32,7 @@ def tile_bitmarmodel_kernel(tc, table, pos, gain, bias, offs, out):
     with (
         tc.tile_pool(name="held", bufs=1) as held,
         tc.tile_pool(name="work", bufs=TOKEN_BLOCKS) as work,
-        tc.psum_pool(name="psum", bufs=2) as psum,
+        tc.psum_pool(name="psum", bufs=TOKEN_BLOCKS - 1) as psum,
     ):
         identity = held.tile([P, P], F32, name="identity")
         masks.make_identity(nc, identity[:])
@@ -70,9 +70,16 @@ def tile_bitmarmodel_kernel(tc, table, pos, gain, bias, offs, out):
 
         for t in range(TOKEN_BLOCKS):
             x = x_blocks[t]
-            x_turned = psum.tile([P, C], F32, name="x_turned", bufs=TOKEN_BLOCKS)
+            last = t == TOKEN_BLOCKS - 1
+            if last:
+                parts = [psum.tile([P, P], F32, name=f"x_last{b}", bufs=1) for b in range(FEATURE_BLOCKS)]
+                x_turned = [part[:] for part in parts]
+            else:
+                x_turned_block = psum.tile([P, C], F32, name="x_turned_block", tag="bank")
+                parts = [x_turned_block]
+                x_turned = [x_turned_block[:, b * P : (b + 1) * P] for b in range(FEATURE_BLOCKS)]
             for b in range(FEATURE_BLOCKS):
-                nc.tensor.transpose(x_turned[:, b * P : (b + 1) * P], x[:, b, :], identity[:])
+                nc.tensor.transpose(x_turned[b], x[:, b, :], identity[:])
 
             y = work.tile([P, C], F32, name="y")
             if t == 0:
@@ -80,31 +87,46 @@ def tile_bitmarmodel_kernel(tc, table, pos, gain, bias, offs, out):
                 rstd, shift = small[:, 0:1], small[:, 1:2]
                 unused = work.tile([P, C], F32, name="unused")
                 neg_mean = work.tile([P, 1], F32, name="neg_mean")
-                nc.scalar.activation(unused[:], x_turned[:], IDENTITY, scale=-1.0 / C, accum_out=neg_mean[:])
+                nc.scalar.activation(unused[:], x_turned_block[:], IDENTITY, scale=-1.0 / C, accum_out=neg_mean[:])
                 squares = work.tile([P, C], F32, name="squares")
                 sum_squares = work.tile([P, 1], F32, name="sum_squares")
-                nc.scalar.activation(squares[:], x_turned[:], SQUARE, bias=neg_mean[:], accum_out=sum_squares[:])
+                nc.scalar.activation(squares[:], x_turned_block[:], SQUARE, bias=neg_mean[:], accum_out=sum_squares[:])
                 nc.scalar.activation(rstd, sum_squares[:], ABS_RECIPROCAL_SQRT, bias=eps[:], scale=1.0 / C)
                 nc.scalar.activation(shift, neg_mean[:], IDENTITY, scale=rstd)
-                nc.scalar.activation(y[:], x_turned[:], IDENTITY, bias=shift, scale=rstd)
+                nc.scalar.activation(y[:], x_turned_block[:], IDENTITY, bias=shift, scale=rstd)
             else:
                 if t == 1:
                     rstds = held.tile([P, TOKEN_BLOCKS - 1], F32, name="rstds", tag="rstd")
                 rstd = rstds[:, t - 1 : t]
-                stats = work.tile([P, 6], F32, name="stats")
-                nc.vector.bn_stats(stats[:], x_turned[:])
+                stats = work.tile([P, 6 * len(parts)], F32, name="stats")
+                for i, part in enumerate(parts):
+                    nc.vector.bn_stats(stats[:, 6 * i : 6 * (i + 1)], part[:])
                 mean_var = work.tile([P, 2], F32, name="mean_var")
                 nc.vector.bn_aggr(mean_var[:], stats[:])
                 nc.scalar.activation(rstd, mean_var[:, 1:2], ABS_RECIPROCAL_SQRT, bias=eps[:])
-                nc.vector.tensor_scalar(y[:], x_turned[:], mean_var[:, 0:1], rstd, SUBTRACT, MULT)
+                width = C // len(parts)
+                for i, part in enumerate(parts):
+                    nc.vector.tensor_scalar(
+                        y[:, i * width : (i + 1) * width], part[:], mean_var[:, 0:1], rstd, SUBTRACT, MULT
+                    )
 
+            if last:
+                y_turned = [psum.tile([P, P], F32, name=f"y_last{b}", tag="bank")[:] for b in range(FEATURE_BLOCKS)]
+            else:
+                y_turned_block = psum.tile([P, FEATURE_BLOCKS, P], F32, name="y_turned_block")
+                y_turned = [y_turned_block[:, b, :] for b in range(FEATURE_BLOCKS)]
+            for b in range(FEATURE_BLOCKS):
+                nc.tensor.transpose(y_turned[b], y[:, b * P : (b + 1) * P], identity[:])
             result = work.tile([P, FEATURE_BLOCKS, P], F32, name="result")
             for b in range(FEATURE_BLOCKS):
-                y_turned = psum.tile([P, P], F32, name=f"y_turned{b}", bufs=2)
-                nc.tensor.transpose(y_turned[:], y[:, b * P : (b + 1) * P], identity[:])
                 gain_b, bias_b = gain_sb[:, b : b + 1], bias_sb[:, b : b + 1]
-                if t < TOKEN_BLOCKS // 2 or b == 0:
-                    nc.scalar.activation(result[:, b, :], y_turned[:], IDENTITY, bias=bias_b, scale=gain_b)
+                if last and b == 1:
+                    nc.vector.tensor_scalar(result[:, b, :], y_turned[b], gain_b, bias_b, MULT, ADD)
                 else:
-                    nc.vector.tensor_scalar(result[:, b, :], y_turned[:], gain_b, bias_b, MULT, ADD)
-            nc.sync.dma_start(out_view[:, :, t * P : (t + 1) * P], result[:])
+                    nc.scalar.activation(result[:, b, :], y_turned[b], IDENTITY, bias=bias_b, scale=gain_b)
+            tokens = slice(t * P, (t + 1) * P)
+            if last:
+                for b in range(FEATURE_BLOCKS):
+                    nc.sync.dma_start(out_view[:, b, tokens], result[:, b, :])
+            else:
+                nc.sync.dma_start(out_view[:, :, tokens], result[:])

@@ -124,9 +124,4 @@ def tile_bitmarmodel_kernel(tc, table, pos, gain, bias, offs, out):
                     nc.vector.tensor_scalar(result[:, b, :], y_turned[b], gain_b, bias_b, MULT, ADD)
                 else:
                     nc.scalar.activation(result[:, b, :], y_turned[b], IDENTITY, bias=bias_b, scale=gain_b)
-            tokens = slice(t * P, (t + 1) * P)
-            if last:
-                for b in range(FEATURE_BLOCKS):
-                    nc.sync.dma_start(out_view[:, b, tokens], result[:, b, :])
-            else:
-                nc.sync.dma_start(out_view[:, :, tokens], result[:])
+            nc.sync.dma_start(out_view[:, :, t * P : (t + 1) * P], result[:])

@@ -104,10 +104,9 @@ def tile_bitmarmodel_kernel(tc, table, pos, gain, bias, offs, out):
                 mean_var = work.tile([P, 2], F32, name="mean_var")
                 nc.vector.bn_aggr(mean_var[:], stats[:])
                 nc.scalar.activation(rstd, mean_var[:, 1:2], ABS_RECIPROCAL_SQRT, bias=eps[:])
-                width = C // len(parts)
-                for i, part in enumerate(parts):
+                for b in range(FEATURE_BLOCKS):
                     nc.vector.tensor_scalar(
-                        y[:, i * width : (i + 1) * width], part[:], mean_var[:, 0:1], rstd, SUBTRACT, MULT
+                        y[:, b * P : (b + 1) * P], x_turned[b], mean_var[:, 0:1], rstd, SUBTRACT, MULT
                     )
 
             if last:

@@ -41,19 +41,18 @@ def tile_bitmarmodel_kernel(tc, table, pos, gain, bias, offs, out):
         table_warm_up = held.tile([P, 1], F32, name="table_warm_up")
         nc.scalar.activation(table_warm_up[:], eps[:], ABS_RECIPROCAL_SQRT)
 
+        windows = [held.tile([P, S], F32, name=f"window{b}") for b in range(FEATURE_BLOCKS)]
         offsets = held.tile([P, N // 16], U16, name="offsets")
-        nc.sync.dma_start(offsets[:], offs)
-        windows = []
         pos_parts = {}
         for first, end in PIECES:
             for b in range(FEATURE_BLOCKS):
                 if first == 0:
-                    window = held.tile([P, S], F32, name=f"window{b}")
-                    nc.sync.dma_start(window[:], table[b * P : (b + 1) * P, :])
-                    windows.append(window)
+                    nc.sync.dma_start(windows[b][:], table[b * P : (b + 1) * P, :])
                 pos_part = held.tile([P, (end - first) * P], F32, name=f"pos{first}_{b}")
                 nc.sync.dma_start(pos_part[:], pos_view[:, b, first * P : end * P])
                 pos_parts[first, b] = pos_part
+                if first == 0 and b == 0:
+                    nc.sync.dma_start(offsets[:], offs)
         gain_sb = held.tile([P, FEATURE_BLOCKS], F32, name="gain_sb")
         bias_sb = held.tile([P, FEATURE_BLOCKS], F32, name="bias_sb")
         with nc.allow_non_contiguous_dma(reason="256 numbers, one to a partition and feature block"):
@@ -109,17 +108,21 @@ def tile_bitmarmodel_kernel(tc, table, pos, gain, bias, offs, out):
                         y[:, b * P : (b + 1) * P], x_turned[b], mean_var[:, 0:1], rstd, SUBTRACT, MULT
                     )
 
-            if last:
-                y_turned = [psum.tile([P, P], F32, name=f"y_last{b}", tag="bank")[:] for b in range(FEATURE_BLOCKS)]
+            shared = t >= TOKEN_BLOCKS // 2
+            if shared:
+                y_turned = [
+                    psum.tile([P, P], F32, name=f"y_shared{b}", tag="back" if last and b == 1 else "bank")[:]
+                    for b in range(FEATURE_BLOCKS)
+                ]
             else:
-                y_turned_block = psum.tile([P, FEATURE_BLOCKS, P], F32, name="y_turned_block")
+                y_turned_block = psum.tile([P, FEATURE_BLOCKS, P], F32, name="y_turned_block", tag="back")
                 y_turned = [y_turned_block[:, b, :] for b in range(FEATURE_BLOCKS)]
             for b in range(FEATURE_BLOCKS):
                 nc.tensor.transpose(y_turned[b], y[:, b * P : (b + 1) * P], identity[:])
             result = work.tile([P, FEATURE_BLOCKS, P], F32, name="result")
             for b in range(FEATURE_BLOCKS):
                 gain_b, bias_b = gain_sb[:, b : b + 1], bias_sb[:, b : b + 1]
-                if last and b == 1:
+                if shared and b == 1:
                     nc.vector.tensor_scalar(result[:, b, :], y_turned[b], gain_b, bias_b, MULT, ADD)
                 else:
                     nc.scalar.activation(result[:, b, :], y_turned[b], IDENTITY, bias=bias_b, scale=gain_b)

@@ -32,7 +32,7 @@ def tile_bitmarmodel_kernel(tc, table, pos, gain, bias, offs, out):
     with (
         tc.tile_pool(name="held", bufs=1) as held,
         tc.tile_pool(name="work", bufs=TOKEN_BLOCKS) as work,
-        tc.psum_pool(name="psum", bufs=TOKEN_BLOCKS - 1) as psum,
+        tc.psum_pool(name="psum", bufs=1) as psum,
     ):
         identity = held.tile([P, P], F32, name="identity")
         masks.make_identity(nc, identity[:])
@@ -70,15 +70,9 @@ def tile_bitmarmodel_kernel(tc, table, pos, gain, bias, offs, out):
         for t in range(TOKEN_BLOCKS):
             x = x_blocks[t]
             last = t == TOKEN_BLOCKS - 1
-            if last:
-                parts = [psum.tile([P, P], F32, name=f"x_last{b}", bufs=1) for b in range(FEATURE_BLOCKS)]
-                x_turned = [part[:] for part in parts]
-            else:
-                x_turned_block = psum.tile([P, C], F32, name="x_turned_block", tag="bank")
-                parts = [x_turned_block]
-                x_turned = [x_turned_block[:, b * P : (b + 1) * P] for b in range(FEATURE_BLOCKS)]
+            x_turned = psum.tile([P, C], F32, name="x_turned", tag="last" if last else "there", bufs=1 if last else 3)
             for b in range(FEATURE_BLOCKS):
-                nc.tensor.transpose(x_turned[b], x[:, b, :], identity[:])
+                nc.tensor.transpose(x_turned[:, b * P : (b + 1) * P], x[:, b, :], identity[:])
 
             y = work.tile([P, C], F32, name="y")
             if t == 0:
@@ -86,36 +80,34 @@ def tile_bitmarmodel_kernel(tc, table, pos, gain, bias, offs, out):
                 rstd, shift = small[:, 0:1], small[:, 1:2]
                 unused = work.tile([P, C], F32, name="unused")
                 neg_mean = work.tile([P, 1], F32, name="neg_mean")
-                nc.scalar.activation(unused[:], x_turned_block[:], IDENTITY, scale=-1.0 / C, accum_out=neg_mean[:])
+                nc.scalar.activation(unused[:], x_turned[:], IDENTITY, scale=-1.0 / C, accum_out=neg_mean[:])
                 squares = work.tile([P, C], F32, name="squares")
                 sum_squares = work.tile([P, 1], F32, name="sum_squares")
-                nc.scalar.activation(squares[:], x_turned_block[:], SQUARE, bias=neg_mean[:], accum_out=sum_squares[:])
+                nc.scalar.activation(squares[:], x_turned[:], SQUARE, bias=neg_mean[:], accum_out=sum_squares[:])
                 nc.scalar.activation(rstd, sum_squares[:], ABS_RECIPROCAL_SQRT, bias=eps[:], scale=1.0 / C)
                 nc.scalar.activation(shift, neg_mean[:], IDENTITY, scale=rstd)
-                nc.scalar.activation(y[:], x_turned_block[:], IDENTITY, bias=shift, scale=rstd)
+                nc.scalar.activation(y[:], x_turned[:], IDENTITY, bias=shift, scale=rstd)
             else:
                 if t == 1:
                     rstds = held.tile([P, TOKEN_BLOCKS - 1], F32, name="rstds", tag="rstd")
                 rstd = rstds[:, t - 1 : t]
-                stats = work.tile([P, 6 * len(parts)], F32, name="stats")
-                for i, part in enumerate(parts):
-                    nc.vector.bn_stats(stats[:, 6 * i : 6 * (i + 1)], part[:])
+                stats = work.tile([P, 6], F32, name="stats")
+                nc.vector.bn_stats(stats[:], x_turned[:])
                 mean_var = work.tile([P, 2], F32, name="mean_var")
                 nc.vector.bn_aggr(mean_var[:], stats[:])
                 nc.scalar.activation(rstd, mean_var[:, 1:2], ABS_RECIPROCAL_SQRT, bias=eps[:])
                 for b in range(FEATURE_BLOCKS):
-                    nc.vector.tensor_scalar(
-                        y[:, b * P : (b + 1) * P], x_turned[b], mean_var[:, 0:1], rstd, SUBTRACT, MULT
-                    )
+                    columns = slice(b * P, (b + 1) * P)
+                    nc.vector.tensor_scalar(y[:, columns], x_turned[:, columns], mean_var[:, 0:1], rstd, SUBTRACT, MULT)
 
             shared = t >= TOKEN_BLOCKS // 2
             if shared:
                 y_turned = [
-                    psum.tile([P, P], F32, name=f"y_shared{b}", tag="back" if last and b == 1 else "bank")[:]
+                    psum.tile([P, P], F32, name=f"y_shared{b}", tag="back" if last and b == 1 else "there", bufs=3)[:]
                     for b in range(FEATURE_BLOCKS)
                 ]
             else:
-                y_turned_block = psum.tile([P, FEATURE_BLOCKS, P], F32, name="y_turned_block", tag="back")
+                y_turned_block = psum.tile([P, FEATURE_BLOCKS, P], F32, name="y_turned_block", tag="back", bufs=3)
                 y_turned = [y_turned_block[:, b, :] for b in range(FEATURE_BLOCKS)]
             for b in range(FEATURE_BLOCKS):
                 nc.tensor.transpose(y_turned[b], y[:, b * P : (b + 1) * P], identity[:])

import concourse.masks as masks
import concourse.mybir as mybir

F32 = mybir.dt.float32
U16 = mybir.dt.uint16
ADD = mybir.AluOpType.add
MULT = mybir.AluOpType.mult
SUBTRACT = mybir.AluOpType.subtract
IDENTITY = mybir.ActivationFunctionType.Identity
ABS_RECIPROCAL_SQRT = mybir.ActivationFunctionType.Abs_reciprocal_sqrt
SQUARE = mybir.ActivationFunctionType.Square

P = 128
C = 256
S = 256
N = 512
EPS = 1e-5
FEATURE_BLOCKS = C // P
TOKEN_BLOCKS = N // P
OFFSET_COLUMNS = P // 16
PIECES = ((0, 1), (1, TOKEN_BLOCKS - 1), (TOKEN_BLOCKS - 1, TOKEN_BLOCKS))


def tile_bitmarmodel_kernel(tc, table, pos, gain, bias, offs, out):
    nc = tc.nc

    pos_view = pos.rearrange("(b p) n -> p b n", p=P)
    out_view = out.rearrange("(b p) n -> p b n", p=P)
    gain_view = gain.rearrange("(b p) o -> p (b o)", p=P)
    bias_view = bias.rearrange("(b p) o -> p (b o)", p=P)

    with (
        tc.tile_pool(name="held", bufs=1) as held,
        tc.tile_pool(name="work", bufs=TOKEN_BLOCKS) as work,
        tc.psum_pool(name="psum", bufs=1) as psum,
    ):
        identity = held.tile([P, P], F32, name="identity")
        masks.make_identity(nc, identity[:])
        eps = held.tile([P, 1], F32, name="eps")
        nc.vector.memset(eps[:], EPS)
        table_warm_up = held.tile([P, 1], F32, name="table_warm_up")
        nc.scalar.activation(table_warm_up[:], eps[:], ABS_RECIPROCAL_SQRT)

        windows = [held.tile([P, S], F32, name=f"window{b}") for b in range(FEATURE_BLOCKS)]
        offsets = held.tile([P, N // 16], U16, name="offsets")
        pos_parts = {}
        for first, end in PIECES:
            for b in range(FEATURE_BLOCKS):
                if first == 0:
                    nc.sync.dma_start(windows[b][:], table[b * P : (b + 1) * P, :])
                pos_part = held.tile([P, (end - first) * P], F32, name=f"pos{first}_{b}")
                nc.sync.dma_start(pos_part[:], pos_view[:, b, first * P : end * P])
                pos_parts[first, b] = pos_part
                if first == 0 and b == 0:
                    nc.sync.dma_start(offsets[:], offs)
        gain_sb = held.tile([P, FEATURE_BLOCKS], F32, name="gain_sb")
        bias_sb = held.tile([P, FEATURE_BLOCKS], F32, name="bias_sb")
        with nc.allow_non_contiguous_dma(reason="256 numbers, one to a partition and feature block"):
            nc.sync.dma_start(gain_sb[:], gain_view)
            nc.sync.dma_start(bias_sb[:], bias_view)

        x_blocks = []
        for first, end in PIECES:
            x = held.tile([P, FEATURE_BLOCKS, (end - first) * P], F32, name=f"x{first}")
            piece = offsets[:, first * OFFSET_COLUMNS : end * OFFSET_COLUMNS]
            for b in range(FEATURE_BLOCKS):
                nc.vector.tensor_tensor(x[:, b, :], windows[b][:].indirect(piece), pos_parts[first, b][:], ADD)
            x_blocks += [x[:, :, i * P : (i + 1) * P] for i in range(end - first)]

        for t in range(TOKEN_BLOCKS):
            x = x_blocks[t]
            last = t == TOKEN_BLOCKS - 1
            x_turned = psum.tile([P, C], F32, name="x_turned", tag="last" if last else "there", bufs=1 if last else 3)
            for b in range(FEATURE_BLOCKS):
                nc.tensor.transpose(x_turned[:, b * P : (b + 1) * P], x[:, b, :], identity[:])

            y = work.tile([P, C], F32, name="y")
            if t == 0:
                small = held.tile([P, 2], F32, name="small", tag="rstd")
                rstd, shift = small[:, 0:1], small[:, 1:2]
                unused = work.tile([P, C], F32, name="unused")
                neg_mean = work.tile([P, 1], F32, name="neg_mean")
                nc.scalar.activation(unused[:], x_turned[:], IDENTITY, scale=-1.0 / C, accum_out=neg_mean[:])
                squares = work.tile([P, C], F32, name="squares")
                sum_squares = work.tile([P, 1], F32, name="sum_squares")
                nc.scalar.activation(squares[:], x_turned[:], SQUARE, bias=neg_mean[:], accum_out=sum_squares[:])
                nc.scalar.activation(rstd, sum_squares[:], ABS_RECIPROCAL_SQRT, bias=eps[:], scale=1.0 / C)
                nc.scalar.activation(shift, neg_mean[:], IDENTITY, scale=rstd)
                nc.scalar.activation(y[:], x_turned[:], IDENTITY, bias=shift, scale=rstd)
            else:
                if t == 1:
                    rstds = held.tile([P, TOKEN_BLOCKS - 1], F32, name="rstds", tag="rstd")
                rstd = rstds[:, t - 1 : t]
                stats = work.tile([P, 6], F32, name="stats")
                nc.vector.bn_stats(stats[:], x_turned[:])
                mean_var = work.tile([P, 2], F32, name="mean_var")
                nc.vector.bn_aggr(mean_var[:], stats[:])
                nc.scalar.activation(rstd, mean_var[:, 1:2], ABS_RECIPROCAL_SQRT, bias=eps[:])
                for b in range(FEATURE_BLOCKS):
                    columns = slice(b * P, (b + 1) * P)
                    nc.vector.tensor_scalar(y[:, columns], x_turned[:, columns], mean_var[:, 0:1], rstd, SUBTRACT, MULT)

            shared = t >= TOKEN_BLOCKS // 2
            if shared:
                y_turned = [
                    psum.tile([P, P], F32, name=f"y_shared{b}", tag="back" if last and b == 1 else "there", bufs=3)[:]
                    for b in range(FEATURE_BLOCKS)
                ]
            else:
                y_turned_block = psum.tile([P, FEATURE_BLOCKS, P], F32, name="y_turned_block", tag="back", bufs=3)
                y_turned = [y_turned_block[:, b, :] for b in range(FEATURE_BLOCKS)]
            for b in range(FEATURE_BLOCKS):
                nc.tensor.transpose(y_turned[b], y[:, b * P : (b + 1) * P], identity[:])
            result = work.tile([P, FEATURE_BLOCKS, P], F32, name="result")
            for b in range(FEATURE_BLOCKS):
                gain_b, bias_b = gain_sb[:, b : b + 1], bias_sb[:, b : b + 1]
                if shared and b == 1:
                    nc.vector.tensor_scalar(result[:, b, :], y_turned[b], gain_b, bias_b, MULT, ADD)
                else:
                    nc.scalar.activation(result[:, b, :], y_turned[b], IDENTITY, bias=bias_b, scale=gain_b)
            nc.sync.dma_start(out_view[:, :, t * P : (t + 1) * P], result[:])
